import numpy as np
import ml_dtypes


def mxq(x, axis, fmt="e4m3"):
    dtype, down = {"e4m3": (ml_dtypes.float8_e4m3fn, 7), "e5m2": (ml_dtypes.float8_e5m2, 14)}[fmt]
    v = np.moveaxis(np.asarray(x, np.float32).astype(ml_dtypes.bfloat16).astype(np.float64), axis, -1)
    blocks = v.reshape(v.shape[:-1] + (-1, 32))
    amax = np.abs(blocks).max(-1, keepdims=True)
    byte = np.maximum(np.where(amax > 0, np.frexp(amax)[1] - 1 + 127, 0) - down, 1)
    scale = np.exp2(byte - 127.0)
    codes = (blocks / scale).astype(np.float32).astype(dtype).astype(np.float64)
    return np.moveaxis((codes * scale).reshape(v.shape), -1, axis)


WIDE = False


def mx_kscale(k):
    if not WIDE:
        return np.ones(k)
    levels = np.array([10, -10, 5, -5, 0])
    if k % 512:
        return np.exp2(np.random.permutation(np.resize(levels, k // 32))).repeat(32)
    a = np.empty((k // 512, 16))
    for p in range(k // 512):
        a[p, :8] = np.random.permutation(np.resize(levels, 8))
        for g in range(8):
            far = levels[np.abs(levels - a[p, g]) >= 10]
            a[p, g + 8] = far[np.random.randint(len(far))]
    return np.exp2(a.ravel()).repeat(32)


BF16 = ml_dtypes.bfloat16


def bf(x):
    return np.asarray(x, np.float32).astype(BF16)


def f64(x):
    return np.asarray(x).astype(np.float64)


B, C, H, W, M, O = 32, 512, 16, 16, 512, 128
N = B * H * W
L2_EPS = 1e-12
BN_EPS = 1e-5


def l2_normalize(x, axis):
    n = np.sqrt(np.sum(x * x, axis=axis, keepdims=True))
    return x / np.maximum(n, L2_EPS)


def setup_inputs():
    s = mx_kscale(C)
    cm = (np.random.standard_normal((N, C)) * 5.0 + np.random.standard_normal((1, C)) * 1.5) / np.sqrt(C)
    w = np.random.standard_normal((O, 2 * C)) * 0.1 / np.sqrt(2 * C)
    w[:, C:] = w[:, C:] / s
    return {"query": bf(np.random.standard_normal((B, C, H, W))), "concat_memory": bf(cm * s), "conv_w": bf(w),
            "bn_gamma": bf(1.0 + 0.1 * np.random.standard_normal(O)), "bn_beta": bf(0.2 * np.random.standard_normal(O))}


def reference(query, concat_memory, conv_w, bn_gamma, bn_beta):
    q_flat = l2_normalize(f64(query), 1).transpose(0, 2, 3, 1).reshape(N, C)
    upd = np.concatenate([q_flat, f64(concat_memory)], axis=1)
    y = mxq(upd, 1, "e4m3") @ mxq(f64(conv_w), 1, "e4m3").T
    y = y.reshape(B, H, W, O).transpose(0, 3, 1, 2)
    mean = np.mean(y, axis=(0, 2, 3), keepdims=True)
    var = np.mean((y - mean) ** 2, axis=(0, 2, 3), keepdims=True)
    y = (y - mean) / np.sqrt(var + BN_EPS)
    y = y * f64(bn_gamma)[None, :, None, None] + f64(bn_beta)[None, :, None, None]
    return np.maximum(y, 0.0)

@@ -1,0 +1,276 @@
+from contextlib import ExitStack
+
+import concourse.mybir as mybir
+from concourse.masks import make_identity
+
+F32 = mybir.dt.float32
+BF16 = mybir.dt.bfloat16
+U32 = mybir.dt.uint32
+U8 = mybir.dt.uint8
+FP8X4 = mybir.dt.float8_e4m3fn_x4
+AF = mybir.ActivationFunctionType
+ALU = mybir.AluOpType
+
+P = 128
+PACK = 4
+GROUPS = 16
+IMAGES = 2
+PIXELS = 256
+GROUP_PIXELS = IMAGES * PIXELS
+FLOPS = 2 * 8192 * 1024 * 128
+
+L2_EPS = 1e-12
+BN_EPS = 1e-5
+
+LOAD_QUERY_AHEAD = 7
+LOAD_MEMORY_AHEAD = 6
+SQUARE_AHEAD = 4
+MEMORY_AHEAD = 3
+SPREAD_AHEAD = 2
+QUANTISE_AHEAD = 1
+MX_BEHIND = 1
+
+SCALAR_STATS = [10, 11, 12, 13]
+VECTOR_STATS = GROUPS - len(SCALAR_STATS)
+
+
+def tile_memory_sup_pb_t_kernel(tc, query, concat_memory, conv_w, bn_gamma, bn_beta, out):
+    nc = tc.nc
+    query_view = query.rearrange("(g b) (p j) h w -> g p b (j h w)", b=IMAGES, j=PACK)
+    memory_view = concat_memory.rearrange("(g b p t) k -> g p b (t k)", b=IMAGES, p=P, t=2)
+    out_view = out.rearrange("(g b) o h w -> g o b (h w)", b=IMAGES)
+
+    with ExitStack() as ctx:
+        ctx.enter_context(tc.manual_schedule())
+        const = ctx.enter_context(tc.tile_pool(name="const", bufs=1))
+        keep = ctx.enter_context(tc.tile_pool(name="keep", bufs=1))
+        query_pool = ctx.enter_context(tc.tile_pool(name="query_pool", bufs=LOAD_QUERY_AHEAD - QUANTISE_AHEAD + 1))
+        memory_pool = ctx.enter_context(tc.tile_pool(name="memory_pool", bufs=LOAD_MEMORY_AHEAD - MEMORY_AHEAD + 1))
+        norm_pool = ctx.enter_context(tc.tile_pool(name="norm_pool", bufs=SQUARE_AHEAD - SPREAD_AHEAD + 1))
+        m_pool = ctx.enter_context(tc.tile_pool(name="m_pool", bufs=MEMORY_AHEAD - QUANTISE_AHEAD + 2))
+        q_pool = ctx.enter_context(tc.tile_pool(name="q_pool", bufs=2))
+        unread_pool = ctx.enter_context(tc.tile_pool(name="unread_pool", bufs=2))
+        psum = ctx.enter_context(tc.psum_pool(name="psum", bufs=2))
+
+        query_tile = {}
+        memory_tile = {}
+        turned_q = {}
+        turned_m = {}
+        squares = {}
+        inv_raw = {}
+        inv_norm = {}
+        spread = {}
+        q_grouped = {}
+        m_grouped = {}
+        q_codes = {}
+        q_scales = {}
+        m_codes = {}
+        m_scales = {}
+        sums = {}
+        bank_of = {}
+
+        one = const.tile([P, 1], F32, name="one")
+        nc.vector.memset(one[:], 1.0)
+        warm = const.tile([P, 1], F32, name="warm")
+        nc.scalar.activation(out=warm[:], in_=one[:], func=AF.Abs_reciprocal_sqrt)
+        ident = const.tile([P, P], F32, name="ident")
+        make_identity(nc, ident[:])
+        gamma = const.tile([P, 1], BF16, name="gamma")
+        beta = const.tile([P, 1], BF16, name="beta")
+        with nc.allow_non_contiguous_dma(reason="one bn parameter per partition"):
+            nc.gpsimd.dma_start(out=gamma[:], in_=bn_gamma.rearrange("(o x) -> o x", x=1))
+            nc.gpsimd.dma_start(out=beta[:], in_=bn_beta.rearrange("(o x) -> o x", x=1))
+        stats = const.tile([P, 6 * VECTOR_STATS + 3 * len(SCALAR_STATS)], F32, name="stats")
+        scalar_triples = stats[:, 6 * VECTOR_STATS:].rearrange("p (k s) -> p k s", s=3)
+        nc.vector.memset(scalar_triples, float(GROUP_PIXELS))
+        totals = const.tile([P, len(SCALAR_STATS)], F32, name="totals")
+        w_tile = const.tile([P, 1024], BF16, name="w_tile")
+        w_grouped = const.tile([P, 2, P, PACK], BF16, name="w_grouped", align_bytes=64)
+        w_codes = const.tile([P, 2 * P], U32, name="w_codes", align_bytes=64)
+        w_scales = const.tile([P, 2 * P], U8, name="w_scales", align_bytes=64)
+        turned_w = psum.tile([P, 4, P], F32, name="turned_w", tag="sums")
+
+        def load_query(g):
+            query_tile[g] = query_pool.tile([P, IMAGES, PACK, PIXELS], BF16, name="query_tile")
+            dst = query_tile[g][:].rearrange("p b j n -> p b (j n)")
+            if g == 0:
+                for b in range(IMAGES):
+                    nc.sync.dma_start(out=dst[:, b], in_=query_view[g][:, b])
+            else:
+                nc.sync.dma_start(out=dst, in_=query_view[g])
+
+        def load_memory(g):
+            memory_tile[g] = memory_pool.tile([P, IMAGES, 2, 512], BF16, name="memory_tile")
+            nc.sync.dma_start(out=memory_tile[g][:].rearrange("p b t k -> p b (t k)"), in_=memory_view[g])
+
+        def turn_weights():
+            words = w_tile[:].bitcast(F32)
+            for h in range(2):
+                nc.tensor.transpose(turned_w[:, h, :], words[:, h:256:2], ident[:])
+            for u in range(2):
+                nc.tensor.transpose(turned_w[:, 2 + u, :], words[:, 256 + u:512:2], ident[:])
+
+        def quantise_weights():
+            nc.vector.tensor_copy(out=w_grouped[:].bitcast(F32),
+                                  in_=turned_w[:].rearrange("p (a h) o -> p a o h", a=2))
+            nc.vector.quantize_mx(out=w_codes[:].bitcast(FP8X4), scales=w_scales[:],
+                                  in_=w_grouped[:].rearrange("p a o t -> p (a o t)"))
+
+        def turn_query(g, b):
+            turned_q[(g, b)] = psum.tile([P, PACK, P], F32, name="turned_q", tag="turned_q")
+            words = query_tile[g][:].bitcast(F32)
+            for j in range(PACK):
+                nc.tensor.transpose(turned_q[(g, b)][:, j, :], words[:, b, j, :], ident[:])
+
+        def sum_squares(g, b):
+            if b == 0:
+                squares[g] = norm_pool.tile([P, 2 * IMAGES], F32, name="squares")
+            halves = turned_q[(g, b)][:].bitcast(BF16).rearrange("w j (p e) -> w j p e", e=2)
+            for parity in range(2):
+                unread = unread_pool.tile([P, PACK, P], BF16, name="unread")
+                nc.scalar.activation(out=unread[:], in_=halves[:, :, :, parity], func=AF.Square,
+                                     accum_out=squares[g][:, 2 * b + parity:2 * b + parity + 1])
+
+        def invert_norm(g):
+            inv_raw[g] = norm_pool.tile([P, 2 * IMAGES], F32, name="inv_raw")
+            nc.scalar.activation(out=inv_raw[g][:], in_=squares[g][:], func=AF.Abs_reciprocal_sqrt)
+            inv_norm[g] = norm_pool.tile([P, 2 * IMAGES], F32, name="inv_norm")
+            nc.gpsimd.tensor_scalar(out=inv_norm[g][:], in0=inv_raw[g][:], scalar1=1.0 / L2_EPS, scalar2=0.0,
+                                    op0=ALU.min, op1=ALU.max)
+
+        def spread_inv_norm(g):
+            spread[g] = psum.tile([P, 2, IMAGES, P], F32, name="spread", tag="spread")
+            for b in range(IMAGES):
+                for parity in range(2):
+                    column = 2 * b + parity
+                    nc.tensor.transpose(spread[g][:, parity, b, :],
+                                        inv_norm[g][:, column:column + 1].to_broadcast([P, P]), ident[:])
+
+        def normalise_query(g):
+            q_grouped[g] = q_pool.tile([P, IMAGES, PIXELS, PACK], BF16, name="q_grouped", align_bytes=64)
+            nc.vector.tensor_tensor(
+                out=q_grouped[g][:].rearrange("p b (w e) j -> p b w e j", e=2),
+                in0=query_tile[g][:].rearrange("p b j (w e) -> p b w e j", e=2),
+                in1=spread[g][:].rearrange("p e b w -> p b w e").unsqueeze(4).to_broadcast([P, IMAGES, P, 2, PACK]),
+                op=ALU.mult,
+            )
+
+        def quantise_query(g):
+            q_codes[g] = keep.tile([P, GROUP_PIXELS], U32, name="q_codes%d" % g, align_bytes=64)
+            q_scales[g] = keep.tile([P, GROUP_PIXELS], U8, name="q_scales%d" % g, align_bytes=64)
+            nc.vector.quantize_mx(out=q_codes[g][:].bitcast(FP8X4), scales=q_scales[g][:],
+                                  in_=q_grouped[g][:].rearrange("p b n j -> p (b n j)"))
+
+        def turn_memory(g, b):
+            turned_m[(g, b)] = psum.tile([P, 2, 2, P], F32, name="turned_m", tag="turned_m")
+            words = memory_tile[g][:].bitcast(F32)
+            for t in range(2):
+                for u in range(2):
+                    nc.tensor.transpose(turned_m[(g, b)][:, u, t, :], words[:, b, t, u:256:2], ident[:])
+
+        def group_memory(g, b):
+            if b == 0:
+                m_grouped[g] = m_pool.tile([P, IMAGES, PIXELS, PACK], BF16, name="m_grouped", align_bytes=64)
+            nc.scalar.copy(
+                out=m_grouped[g][:].bitcast(F32)[:, b].rearrange("p (r t) u -> p r t u", t=2),
+                in_=turned_m[(g, b)][:].rearrange("p u t r -> p r t u"),
+            )
+
+        def quantise_memory(g):
+            m_codes[g] = keep.tile([P, GROUP_PIXELS], U32, name="m_codes%d" % g, align_bytes=64)
+            m_scales[g] = keep.tile([P, GROUP_PIXELS], U8, name="m_scales%d" % g, align_bytes=64)
+            nc.vector.quantize_mx(out=m_codes[g][:].bitcast(FP8X4), scales=m_scales[g][:],
+                                  in_=m_grouped[g][:].rearrange("p b n j -> p (b n j)"))
+
+        def multiply(g, kind):
+            sums[g] = psum.tile([P, GROUP_PIXELS], F32, name="sums", tag=kind)
+            bank_of[g] = kind
+            nc.tensor.matmul_mx(out=sums[g][:], lhsT=w_codes[:, 0:P].bitcast(FP8X4), lhsT_scale=w_scales[:, 0:P],
+                                rhs=q_codes[g][:].bitcast(FP8X4), rhs_scale=q_scales[g][:], start=True, stop=False)
+            nc.tensor.matmul_mx(out=sums[g][:], lhsT=w_codes[:, P:2 * P].bitcast(FP8X4),
+                                lhsT_scale=w_scales[:, P:2 * P],
+                                rhs=m_codes[g][:].bitcast(FP8X4), rhs_scale=m_scales[g][:], start=False, stop=True)
+
+        def first_bank(g):
+            if g < GROUPS - 4:
+                return "sums"
+            if g < GROUPS - 2:
+                return "turned_q"
+            return "turned_m"
+
+        def take_statistics(g):
+            if g in SCALAR_STATS:
+                k = SCALAR_STATS.index(g)
+                unread = unread_pool.tile([P, GROUP_PIXELS], BF16, name="unread")
+                nc.scalar.activation(out=unread[:], in_=sums[g][:], func=AF.Identity, accum_out=totals[:, k:k + 1])
+                nc.scalar.mul(out=scalar_triples[:, k, 1:2], in_=totals[:, k:k + 1], mul=1.0 / GROUP_PIXELS)
+                unread = unread_pool.tile([P, GROUP_PIXELS], BF16, name="unread")
+                nc.scalar.activation(out=unread[:], in_=sums[g][:], func=AF.Square, scale=-1.0,
+                                     bias=scalar_triples[:, k, 1:2], accum_out=scalar_triples[:, k, 2:3])
+            else:
+                slot = g if g < SCALAR_STATS[0] else g - len(SCALAR_STATS)
+                nc.vector.bn_stats(out=stats[:, 6 * slot:6 * slot + 6], in_=sums[g][:])
+
+        def is_group(g):
+            return 0 <= g < GROUPS
+
+        for rnd in range(-LOAD_QUERY_AHEAD, GROUPS + MX_BEHIND):
+            if is_group(rnd + LOAD_MEMORY_AHEAD):
+                load_memory(rnd + LOAD_MEMORY_AHEAD)
+            if is_group(rnd + LOAD_QUERY_AHEAD):
+                load_query(rnd + LOAD_QUERY_AHEAD)
+            if rnd == -LOAD_QUERY_AHEAD:
+                nc.sync.dma_start(out=w_tile[:], in_=conv_w)
+            if is_group(rnd + SPREAD_AHEAD) and rnd + SPREAD_AHEAD > 0:
+                spread_inv_norm(rnd + SPREAD_AHEAD)
+            if is_group(rnd - MX_BEHIND):
+                multiply(rnd - MX_BEHIND, first_bank(rnd - MX_BEHIND))
+            if rnd >= GROUPS - 1:
+                multiply(rnd - (GROUPS - 1), "spread")
+            if is_group(rnd + QUANTISE_AHEAD):
+                normalise_query(rnd + QUANTISE_AHEAD)
+            for b in range(IMAGES):
+                if is_group(rnd + SQUARE_AHEAD):
+                    turn_query(rnd + SQUARE_AHEAD, b)
+                    sum_squares(rnd + SQUARE_AHEAD, b)
+                if is_group(rnd + MEMORY_AHEAD):
+                    turn_memory(rnd + MEMORY_AHEAD, b)
+                    group_memory(rnd + MEMORY_AHEAD, b)
+                if rnd == -SPREAD_AHEAD - 1 and b == 0:
+                    spread_inv_norm(0)
+            if rnd == -SQUARE_AHEAD:
+                turn_weights()
+                quantise_weights()
+            if is_group(rnd + SQUARE_AHEAD):
+                invert_norm(rnd + SQUARE_AHEAD)
+            if is_group(rnd + QUANTISE_AHEAD):
+                quantise_memory(rnd + QUANTISE_AHEAD)
+                quantise_query(rnd + QUANTISE_AHEAD)
+            if is_group(rnd - MX_BEHIND):
+                take_statistics(rnd - MX_BEHIND)
+
+        mean_var = const.tile([P, 2], F32, name="mean_var")
+        nc.vector.bn_aggr(out=mean_var[:], in_=stats[:])
+        neg_mean = const.tile([P, 1], F32, name="neg_mean")
+        nc.vector.tensor_scalar_mul(out=neg_mean[:], in0=mean_var[:, 0:1], scalar1=-1.0)
+        rstd = const.tile([P, 1], F32, name="rstd")
+        nc.scalar.activation(out=rstd[:], in_=mean_var[:, 1:2], func=AF.Abs_reciprocal_sqrt, bias=BN_EPS)
+        scale = const.tile([P, 1], F32, name="scale")
+        nc.scalar.mul(out=scale[:], in_=gamma[:], mul=rstd[:, 0:1])
+        shift = const.tile([P, 1], F32, name="shift")
+        nc.scalar.activation(out=shift[:], in_=scale[:], func=AF.Identity, bias=beta[:, 0:1], scale=neg_mean[:, 0:1])
+
+        in_psum = list(range(GROUPS - 6, GROUPS)) + [0, 1]
+        again = list(range(2, GROUPS - 6))
+        for n, g in enumerate(in_psum + again):
+            result = keep.tile([P, GROUP_PIXELS], F32, name="result%d" % g)
+            if n % 3 == 1:
+                nc.vector.tensor_scalar(out=result[:], in0=sums[g][:], scalar1=scale[:, 0:1], scalar2=shift[:, 0:1],
+                                        op0=ALU.mult, op1=ALU.add)
+                nc.vector.tensor_scalar_max(out=result[:], in0=result[:], scalar1=0.0)
+            else:
+                nc.scalar.activation(out=result[:], in_=sums[g][:], func=AF.Relu, bias=shift[:, 0:1],
+                                     scale=scale[:, 0:1])
+            nc.sync.dma_start(out=out_view[g], in_=result[:].rearrange("o (b n) -> o b n", b=IMAGES))
+            if n < len(again):
+                multiply(again[n], bank_of[g])

@@ -16,6 +16,7 @@ PACK = 4
 GROUPS = 16
 IMAGES = 2
 PIXELS = 256
+RUN = 4
 GROUP_PIXELS = IMAGES * PIXELS
 FLOPS = 2 * 8192 * 1024 * 128
 
@@ -139,21 +140,23 @@ def tile_memory_sup_pb_t_kernel(tc, query, concat_memory, conv_w, bn_gamma, bn_b
                                     op0=ALU.min, op1=ALU.max)
 
         def spread_inv_norm(g):
-            spread[g] = psum.tile([P, 2, IMAGES, P], F32, name="spread", tag="spread")
+            spread[g] = psum.tile([P, IMAGES, PIXELS], F32, name="spread", tag="spread")
             for b in range(IMAGES):
                 for parity in range(2):
                     column = 2 * b + parity
-                    nc.tensor.transpose(spread[g][:, parity, b, :],
+                    nc.tensor.transpose(spread[g][:, b, parity:PIXELS:2],
                                         inv_norm[g][:, column:column + 1].to_broadcast([P, P]), ident[:])
 
         def normalise_query(g):
             q_grouped[g] = q_pool.tile([P, IMAGES, PIXELS, PACK], BF16, name="q_grouped", align_bytes=64)
-            nc.vector.tensor_tensor(
-                out=q_grouped[g][:].rearrange("p b (w e) j -> p b w e j", e=2),
-                in0=query_tile[g][:].rearrange("p b j (w e) -> p b w e j", e=2),
-                in1=spread[g][:].rearrange("p e b w -> p b w e").unsqueeze(4).to_broadcast([P, IMAGES, P, 2, PACK]),
-                op=ALU.mult,
-            )
+            for b in range(IMAGES):
+                nc.vector.tensor_tensor(
+                    out=q_grouped[g][:, b].rearrange("p (c i) j -> p c j i", i=RUN),
+                    in0=query_tile[g][:, b].rearrange("p j (c i) -> p c j i", i=RUN),
+                    in1=spread[g][:, b].rearrange("p (c i) -> p c i", i=RUN).unsqueeze(2).to_broadcast(
+                        [P, PIXELS // RUN, PACK, RUN]),
+                    op=ALU.mult,
+                )
 
         def quantise_query(g):
             q_codes[g] = keep.tile([P, GROUP_PIXELS], U32, name="q_codes%d" % g, align_bytes=64)

@@ -31,7 +31,7 @@ SPREAD_AHEAD = 2
 QUANTISE_AHEAD = 1
 MX_BEHIND = 1
 
-SCALAR_STATS = [10, 11, 12, 13]
+SCALAR_STATS = [8, 9, 10, 11, 12, 13]
 VECTOR_STATS = GROUPS - len(SCALAR_STATS)
 
 
@@ -132,16 +132,19 @@ def tile_memory_sup_pb_t_kernel(tc, query, concat_memory, conv_w, bn_gamma, bn_b
                 nc.scalar.activation(out=unread[:], in_=halves[:, :, :, parity], func=AF.Square,
                                      accum_out=squares[g][:, 2 * b + parity:2 * b + parity + 1])
 
-        def invert_norm(g):
-            inv_raw[g] = norm_pool.tile([P, 2 * IMAGES], F32, name="inv_raw")
-            nc.scalar.activation(out=inv_raw[g][:], in_=squares[g][:], func=AF.Abs_reciprocal_sqrt)
-            inv_norm[g] = norm_pool.tile([P, 2 * IMAGES], F32, name="inv_norm")
-            nc.gpsimd.tensor_scalar(out=inv_norm[g][:], in0=inv_raw[g][:], scalar1=1.0 / L2_EPS, scalar2=0.0,
-                                    op0=ALU.min, op1=ALU.max)
+        def invert_norm(g, images):
+            if images[0] == 0:
+                inv_raw[g] = norm_pool.tile([P, 2 * IMAGES], F32, name="inv_raw")
+                inv_norm[g] = norm_pool.tile([P, 2 * IMAGES], F32, name="inv_norm")
+            columns = slice(2 * images[0], 2 * images[-1] + 2)
+            nc.scalar.activation(out=inv_raw[g][:, columns], in_=squares[g][:, columns], func=AF.Abs_reciprocal_sqrt)
+            nc.gpsimd.tensor_scalar(out=inv_norm[g][:, columns], in0=inv_raw[g][:, columns], scalar1=1.0 / L2_EPS,
+                                    scalar2=0.0, op0=ALU.min, op1=ALU.max)
 
-        def spread_inv_norm(g):
-            spread[g] = psum.tile([P, IMAGES, PIXELS], F32, name="spread", tag="spread")
-            for b in range(IMAGES):
+        def spread_inv_norm(g, images):
+            if images[0] == 0:
+                spread[g] = psum.tile([P, IMAGES, PIXELS], F32, name="spread", tag="spread")
+            for b in images:
                 for parity in range(2):
                     column = 2 * b + parity
                     nc.tensor.transpose(spread[g][:, b, parity:PIXELS:2],
@@ -174,7 +177,8 @@ def tile_memory_sup_pb_t_kernel(tc, query, concat_memory, conv_w, bn_gamma, bn_b
         def group_memory(g, b):
             if b == 0:
                 m_grouped[g] = m_pool.tile([P, IMAGES, PIXELS, PACK], BF16, name="m_grouped", align_bytes=64)
-            nc.scalar.copy(
+            copy = nc.vector.tensor_copy if g == 0 else nc.scalar.copy
+            copy(
                 out=m_grouped[g][:].bitcast(F32)[:, b].rearrange("p (r t) u -> p r t u", t=2),
                 in_=turned_m[(g, b)][:].rearrange("p u t r -> p r t u"),
             )
@@ -217,15 +221,28 @@ def tile_memory_sup_pb_t_kernel(tc, query, concat_memory, conv_w, bn_gamma, bn_b
         def is_group(g):
             return 0 <= g < GROUPS
 
+        both = range(IMAGES)
+        load_query(0)
+        nc.sync.dma_start(out=w_tile[:], in_=conv_w)
+        load_memory(0)
+        for b in both:
+            turn_query(0, b)
+            sum_squares(0, b)
+            invert_norm(0, [b])
+        turn_weights()
+        quantise_weights()
+        for b in both:
+            turn_memory(0, b)
+            group_memory(0, b)
+        spread_inv_norm(0, [0])
+        quantise_memory(0)
         for rnd in range(-LOAD_QUERY_AHEAD, GROUPS + MX_BEHIND):
-            if is_group(rnd + LOAD_MEMORY_AHEAD):
+            if 0 < rnd + LOAD_MEMORY_AHEAD < GROUPS:
                 load_memory(rnd + LOAD_MEMORY_AHEAD)
-            if is_group(rnd + LOAD_QUERY_AHEAD):
+            if 0 < rnd + LOAD_QUERY_AHEAD < GROUPS:
                 load_query(rnd + LOAD_QUERY_AHEAD)
-            if rnd == -LOAD_QUERY_AHEAD:
-                nc.sync.dma_start(out=w_tile[:], in_=conv_w)
-            if is_group(rnd + SPREAD_AHEAD) and rnd + SPREAD_AHEAD > 0:
-                spread_inv_norm(rnd + SPREAD_AHEAD)
+            if 0 < rnd + SPREAD_AHEAD < GROUPS:
+                spread_inv_norm(rnd + SPREAD_AHEAD, both)
             if is_group(rnd - MX_BEHIND):
                 multiply(rnd - MX_BEHIND, first_bank(rnd - MX_BEHIND))
             if rnd >= GROUPS - 1:
@@ -233,21 +250,19 @@ def tile_memory_sup_pb_t_kernel(tc, query, concat_memory, conv_w, bn_gamma, bn_b
             if is_group(rnd + QUANTISE_AHEAD):
                 normalise_query(rnd + QUANTISE_AHEAD)
             for b in range(IMAGES):
-                if is_group(rnd + SQUARE_AHEAD):
+                if 0 < rnd + SQUARE_AHEAD < GROUPS:
                     turn_query(rnd + SQUARE_AHEAD, b)
                     sum_squares(rnd + SQUARE_AHEAD, b)
-                if is_group(rnd + MEMORY_AHEAD):
+                if rnd + SQUARE_AHEAD == 1 and b == 0:
+                    spread_inv_norm(0, [1])
+                if 0 < rnd + MEMORY_AHEAD < GROUPS:
                     turn_memory(rnd + MEMORY_AHEAD, b)
                     group_memory(rnd + MEMORY_AHEAD, b)
-                if rnd == -SPREAD_AHEAD - 1 and b == 0:
-                    spread_inv_norm(0)
-            if rnd == -SQUARE_AHEAD:
-                turn_weights()
-                quantise_weights()
-            if is_group(rnd + SQUARE_AHEAD):
-                invert_norm(rnd + SQUARE_AHEAD)
+            if 0 < rnd + SQUARE_AHEAD < GROUPS:
+                invert_norm(rnd + SQUARE_AHEAD, both)
             if is_group(rnd + QUANTISE_AHEAD):
-                quantise_memory(rnd + QUANTISE_AHEAD)
+                if rnd + QUANTISE_AHEAD > 0:
+                    quantise_memory(rnd + QUANTISE_AHEAD)
                 quantise_query(rnd + QUANTISE_AHEAD)
             if is_group(rnd - MX_BEHIND):
                 take_statistics(rnd - MX_BEHIND)

@@ -24,12 +24,14 @@ L2_EPS = 1e-12
 BN_EPS = 1e-5
 
 LOAD_QUERY_AHEAD = 7
-LOAD_MEMORY_AHEAD = 6
+LOAD_MEMORY_AHEAD = 5
 SQUARE_AHEAD = 4
 MEMORY_AHEAD = 3
 SPREAD_AHEAD = 2
 QUANTISE_AHEAD = 1
 MX_BEHIND = 1
+
+BY_MATMUL = [(0, 0), (0, 1)]
 
 SCALAR_STATS = [8, 9, 10, 11, 12, 13]
 VECTOR_STATS = GROUPS - len(SCALAR_STATS)
@@ -39,7 +41,6 @@ def tile_memory_sup_pb_t_kernel(tc, query, concat_memory, conv_w, bn_gamma, bn_b
     nc = tc.nc
     query_view = query.rearrange("(g b) (p j) h w -> g p b (j h w)", b=IMAGES, j=PACK)
     memory_view = concat_memory.rearrange("(g b p t) k -> g p b (t k)", b=IMAGES, p=P, t=2)
-    out_view = out.rearrange("(g b) o h w -> g o b (h w)", b=IMAGES)
 
     with ExitStack() as ctx:
         ctx.enter_context(tc.manual_schedule())
@@ -56,6 +57,7 @@ def tile_memory_sup_pb_t_kernel(tc, query, concat_memory, conv_w, bn_gamma, bn_b
         query_tile = {}
         memory_tile = {}
         turned_q = {}
+        gram = {}
         turned_m = {}
         squares = {}
         inv_raw = {}
@@ -85,6 +87,7 @@ def tile_memory_sup_pb_t_kernel(tc, query, concat_memory, conv_w, bn_gamma, bn_b
         scalar_triples = stats[:, 6 * VECTOR_STATS:].rearrange("p (k s) -> p k s", s=3)
         nc.vector.memset(scalar_triples, float(GROUP_PIXELS))
         totals = const.tile([P, len(SCALAR_STATS)], F32, name="totals")
+        deviations = const.tile([P, len(SCALAR_STATS)], F32, name="deviations")
         w_tile = const.tile([P, 1024], BF16, name="w_tile")
         w_grouped = const.tile([P, 2, P, PACK], BF16, name="w_grouped", align_bytes=64)
         w_codes = const.tile([P, 2 * P], U32, name="w_codes", align_bytes=64)
@@ -117,6 +120,14 @@ def tile_memory_sup_pb_t_kernel(tc, query, concat_memory, conv_w, bn_gamma, bn_b
             nc.vector.quantize_mx(out=w_codes[:].bitcast(FP8X4), scales=w_scales[:],
                                   in_=w_grouped[:].rearrange("p a o t -> p (a o t)"))
 
+        def measure_query(g, b):
+            if (g, b) in BY_MATMUL:
+                gram_query(g, b)
+                sum_squares_from_gram(g, b)
+            else:
+                turn_query(g, b)
+                sum_squares(g, b)
+
         def turn_query(g, b):
             turned_q[(g, b)] = psum.tile([P, PACK, P], F32, name="turned_q", tag="turned_q")
             words = query_tile[g][:].bitcast(F32)
@@ -132,6 +143,22 @@ def tile_memory_sup_pb_t_kernel(tc, query, concat_memory, conv_w, bn_gamma, bn_b
                 nc.scalar.activation(out=unread[:], in_=halves[:, :, :, parity], func=AF.Square,
                                      accum_out=squares[g][:, 2 * b + parity:2 * b + parity + 1])
 
+        def gram_query(g, b):
+            gram[(g, b)] = psum.tile([P, 2, P], F32, name="gram", tag="turned_q")
+            for h in range(2):
+                for j in range(PACK):
+                    pixels = query_tile[g][:, b, j, P * h:P * h + P]
+                    nc.tensor.matmul(gram[(g, b)][:, h, :], lhsT=pixels, rhs=pixels, start=(j == 0), stop=(j == PACK - 1))
+
+        def sum_squares_from_gram(g, b):
+            if b == 0:
+                squares[g] = norm_pool.tile([P, 2 * IMAGES], F32, name="squares")
+            for h in range(2):
+                unread_diagonal = unread_pool.tile([P, P], F32, name="unread_diagonal")
+                nc.vector.scalar_tensor_tensor(out=unread_diagonal[:], in0=gram[(g, b)][:, h, :], scalar=1.0, in1=ident[:],
+                                               op0=ALU.mult, op1=ALU.mult,
+                                               accum_out=squares[g][:, 2 * b + h:2 * b + h + 1])
+
         def invert_norm(g, images):
             if images[0] == 0:
                 inv_raw[g] = norm_pool.tile([P, 2 * IMAGES], F32, name="inv_raw")
@@ -142,12 +169,13 @@ def tile_memory_sup_pb_t_kernel(tc, query, concat_memory, conv_w, bn_gamma, bn_b
                                     scalar2=0.0, op0=ALU.min, op1=ALU.max)
 
         def spread_inv_norm(g, images):
-            if images[0] == 0:
-                spread[g] = psum.tile([P, IMAGES, PIXELS], F32, name="spread", tag="spread")
+            spread_tile = psum.tile([P, len(images), PIXELS], F32, name="spread_tile", tag="spread")
             for b in images:
-                for parity in range(2):
-                    column = 2 * b + parity
-                    nc.tensor.transpose(spread[g][:, b, parity:PIXELS:2],
+                spread[(g, b)] = spread_tile[:, b - images[0]]
+                for half in range(2):
+                    column = 2 * b + half
+                    pixels = slice(P * half, P * half + P) if (g, b) in gram else slice(half, PIXELS, 2)
+                    nc.tensor.transpose(spread[(g, b)][:, pixels],
                                         inv_norm[g][:, column:column + 1].to_broadcast([P, P]), ident[:])
 
         def normalise_query(g):
@@ -156,7 +184,7 @@ def tile_memory_sup_pb_t_kernel(tc, query, concat_memory, conv_w, bn_gamma, bn_b
                 nc.vector.tensor_tensor(
                     out=q_grouped[g][:, b].rearrange("p (c i) j -> p c j i", i=RUN),
                     in0=query_tile[g][:, b].rearrange("p j (c i) -> p c j i", i=RUN),
-                    in1=spread[g][:, b].rearrange("p (c i) -> p c i", i=RUN).unsqueeze(2).to_broadcast(
+                    in1=spread[(g, b)].rearrange("p (c i) -> p c i", i=RUN).unsqueeze(2).to_broadcast(
                         [P, PIXELS // RUN, PACK, RUN]),
                     op=ALU.mult,
                 )
@@ -177,8 +205,7 @@ def tile_memory_sup_pb_t_kernel(tc, query, concat_memory, conv_w, bn_gamma, bn_b
         def group_memory(g, b):
             if b == 0:
                 m_grouped[g] = m_pool.tile([P, IMAGES, PIXELS, PACK], BF16, name="m_grouped", align_bytes=64)
-            copy = nc.vector.tensor_copy if g == 0 else nc.scalar.copy
-            copy(
+            nc.scalar.copy(
                 out=m_grouped[g][:].bitcast(F32)[:, b].rearrange("p (r t) u -> p r t u", t=2),
                 in_=turned_m[(g, b)][:].rearrange("p u t r -> p r t u"),
             )
@@ -192,11 +219,11 @@ def tile_memory_sup_pb_t_kernel(tc, query, concat_memory, conv_w, bn_gamma, bn_b
         def multiply(g, kind):
             sums[g] = psum.tile([P, GROUP_PIXELS], F32, name="sums", tag=kind)
             bank_of[g] = kind
-            nc.tensor.matmul_mx(out=sums[g][:], lhsT=w_codes[:, 0:P].bitcast(FP8X4), lhsT_scale=w_scales[:, 0:P],
-                                rhs=q_codes[g][:].bitcast(FP8X4), rhs_scale=q_scales[g][:], start=True, stop=False)
             nc.tensor.matmul_mx(out=sums[g][:], lhsT=w_codes[:, P:2 * P].bitcast(FP8X4),
                                 lhsT_scale=w_scales[:, P:2 * P],
-                                rhs=m_codes[g][:].bitcast(FP8X4), rhs_scale=m_scales[g][:], start=False, stop=True)
+                                rhs=m_codes[g][:].bitcast(FP8X4), rhs_scale=m_scales[g][:], start=True, stop=False)
+            nc.tensor.matmul_mx(out=sums[g][:], lhsT=w_codes[:, 0:P].bitcast(FP8X4), lhsT_scale=w_scales[:, 0:P],
+                                rhs=q_codes[g][:].bitcast(FP8X4), rhs_scale=q_scales[g][:], start=False, stop=True)
 
         def first_bank(g):
             if g < GROUPS - 4:
@@ -205,90 +232,119 @@ def tile_memory_sup_pb_t_kernel(tc, query, concat_memory, conv_w, bn_gamma, bn_b
                 return "turned_q"
             return "turned_m"
 
+        def sum_group(g):
+            k = SCALAR_STATS.index(g)
+            unread = unread_pool.tile([P, GROUP_PIXELS], BF16, name="unread")
+            nc.scalar.activation(out=unread[:], in_=sums[g][:], func=AF.Identity, accum_out=totals[:, k:k + 1])
+
+        def sum_deviations(g):
+            k = SCALAR_STATS.index(g)
+            unread = unread_pool.tile([P, GROUP_PIXELS], BF16, name="unread")
+            nc.scalar.activation(out=unread[:], in_=sums[g][:], func=AF.Square, scale=-float(GROUP_PIXELS),
+                                 bias=totals[:, k:k + 1], accum_out=deviations[:, k:k + 1])
+
+        def gather_statistics():
+            nc.vector.tensor_scalar_mul(out=scalar_triples[:, :, 1], in0=totals[:], scalar1=1.0 / GROUP_PIXELS)
+            nc.vector.tensor_scalar_mul(out=scalar_triples[:, :, 2], in0=deviations[:],
+                                        scalar1=1.0 / (GROUP_PIXELS * GROUP_PIXELS))
+
         def take_statistics(g):
-            if g in SCALAR_STATS:
-                k = SCALAR_STATS.index(g)
-                unread = unread_pool.tile([P, GROUP_PIXELS], BF16, name="unread")
-                nc.scalar.activation(out=unread[:], in_=sums[g][:], func=AF.Identity, accum_out=totals[:, k:k + 1])
-                nc.scalar.mul(out=scalar_triples[:, k, 1:2], in_=totals[:, k:k + 1], mul=1.0 / GROUP_PIXELS)
-                unread = unread_pool.tile([P, GROUP_PIXELS], BF16, name="unread")
-                nc.scalar.activation(out=unread[:], in_=sums[g][:], func=AF.Square, scale=-1.0,
-                                     bias=scalar_triples[:, k, 1:2], accum_out=scalar_triples[:, k, 2:3])
-            else:
-                slot = g if g < SCALAR_STATS[0] else g - len(SCALAR_STATS)
-                nc.vector.bn_stats(out=stats[:, 6 * slot:6 * slot + 6], in_=sums[g][:])
+            slot = g if g < SCALAR_STATS[0] else g - len(SCALAR_STATS)
+            nc.vector.bn_stats(out=stats[:, 6 * slot:6 * slot + 6], in_=sums[g][:])
 
         def is_group(g):
             return 0 <= g < GROUPS
 
         both = range(IMAGES)
         load_query(0)
+        load_query(1)
         nc.sync.dma_start(out=w_tile[:], in_=conv_w)
         load_memory(0)
         for b in both:
-            turn_query(0, b)
-            sum_squares(0, b)
+            measure_query(0, b)
             invert_norm(0, [b])
+        measure_query(1, 0)
+        spread_inv_norm(0, [0])
+        spread_inv_norm(0, [1])
+        measure_query(1, 1)
+        invert_norm(1, both)
         turn_weights()
+        normalise_query(0)
         quantise_weights()
         for b in both:
             turn_memory(0, b)
             group_memory(0, b)
-        spread_inv_norm(0, [0])
-        quantise_memory(0)
         for rnd in range(-LOAD_QUERY_AHEAD, GROUPS + MX_BEHIND):
             if 0 < rnd + LOAD_MEMORY_AHEAD < GROUPS:
                 load_memory(rnd + LOAD_MEMORY_AHEAD)
-            if 0 < rnd + LOAD_QUERY_AHEAD < GROUPS:
+            if 1 < rnd + LOAD_QUERY_AHEAD < GROUPS:
                 load_query(rnd + LOAD_QUERY_AHEAD)
-            if 0 < rnd + SPREAD_AHEAD < GROUPS:
+            if 1 < rnd + SPREAD_AHEAD < GROUPS:
                 spread_inv_norm(rnd + SPREAD_AHEAD, both)
             if is_group(rnd - MX_BEHIND):
                 multiply(rnd - MX_BEHIND, first_bank(rnd - MX_BEHIND))
             if rnd >= GROUPS - 1:
                 multiply(rnd - (GROUPS - 1), "spread")
-            if is_group(rnd + QUANTISE_AHEAD):
+            if 0 < rnd + QUANTISE_AHEAD < GROUPS:
                 normalise_query(rnd + QUANTISE_AHEAD)
             for b in range(IMAGES):
-                if 0 < rnd + SQUARE_AHEAD < GROUPS:
-                    turn_query(rnd + SQUARE_AHEAD, b)
-                    sum_squares(rnd + SQUARE_AHEAD, b)
-                if rnd + SQUARE_AHEAD == 1 and b == 0:
-                    spread_inv_norm(0, [1])
+                if 1 < rnd + SQUARE_AHEAD < GROUPS:
+                    measure_query(rnd + SQUARE_AHEAD, b)
+                if rnd + SQUARE_AHEAD == 2 and b == 0:
+                    spread_inv_norm(1, both)
+                if b == 1 and rnd - MX_BEHIND in SCALAR_STATS:
+                    sum_group(rnd - MX_BEHIND)
                 if 0 < rnd + MEMORY_AHEAD < GROUPS:
                     turn_memory(rnd + MEMORY_AHEAD, b)
                     group_memory(rnd + MEMORY_AHEAD, b)
-            if 0 < rnd + SQUARE_AHEAD < GROUPS:
+            if 1 < rnd + SQUARE_AHEAD < GROUPS:
                 invert_norm(rnd + SQUARE_AHEAD, both)
             if is_group(rnd + QUANTISE_AHEAD):
-                if rnd + QUANTISE_AHEAD > 0:
+                if rnd + QUANTISE_AHEAD == 0:
+                    quantise_query(0)
+                    quantise_memory(0)
+                else:
                     quantise_memory(rnd + QUANTISE_AHEAD)
-                quantise_query(rnd + QUANTISE_AHEAD)
-            if is_group(rnd - MX_BEHIND):
+                    quantise_query(rnd + QUANTISE_AHEAD)
+            if rnd - MX_BEHIND in SCALAR_STATS:
+                if rnd - MX_BEHIND == SCALAR_STATS[-1]:
+                    sum_deviations(SCALAR_STATS[-2])
+                if rnd - MX_BEHIND != SCALAR_STATS[-2]:
+                    sum_deviations(rnd - MX_BEHIND)
+            elif is_group(rnd - MX_BEHIND):
+                if rnd - MX_BEHIND == GROUPS - 1:
+                    gather_statistics()
                 take_statistics(rnd - MX_BEHIND)
 
         mean_var = const.tile([P, 2], F32, name="mean_var")
         nc.vector.bn_aggr(out=mean_var[:], in_=stats[:])
-        neg_mean = const.tile([P, 1], F32, name="neg_mean")
-        nc.vector.tensor_scalar_mul(out=neg_mean[:], in0=mean_var[:, 0:1], scalar1=-1.0)
+        neg_mean_gamma = const.tile([P, 1], F32, name="neg_mean_gamma")
+        nc.vector.scalar_tensor_tensor(out=neg_mean_gamma[:], in0=mean_var[:, 0:1], scalar=-1.0, in1=gamma[:],
+                                       op0=ALU.mult, op1=ALU.mult)
         rstd = const.tile([P, 1], F32, name="rstd")
         nc.scalar.activation(out=rstd[:], in_=mean_var[:, 1:2], func=AF.Abs_reciprocal_sqrt, bias=BN_EPS)
         scale = const.tile([P, 1], F32, name="scale")
         nc.scalar.mul(out=scale[:], in_=gamma[:], mul=rstd[:, 0:1])
         shift = const.tile([P, 1], F32, name="shift")
-        nc.scalar.activation(out=shift[:], in_=scale[:], func=AF.Identity, bias=beta[:, 0:1], scale=neg_mean[:, 0:1])
+        nc.scalar.activation(out=shift[:], in_=neg_mean_gamma[:], func=AF.Identity, bias=beta[:, 0:1], scale=rstd[:, 0:1])
 
         in_psum = list(range(GROUPS - 6, GROUPS)) + [0, 1]
         again = list(range(2, GROUPS - 6))
+        store_view = out.rearrange("n o h w -> o n (h w)")
+        store_after = {10: 10, 11: 11, 13: 12, 15: 14, 1: 0, 5: 2, 9: 6}
+        results = keep.tile([P, GROUPS, IMAGES, PIXELS], F32, name="results")
         for n, g in enumerate(in_psum + again):
-            result = keep.tile([P, GROUP_PIXELS], F32, name="result%d" % g)
+            result = results[:, g].rearrange("o b n -> o (b n)")
             if n % 3 == 1:
-                nc.vector.tensor_scalar(out=result[:], in0=sums[g][:], scalar1=scale[:, 0:1], scalar2=shift[:, 0:1],
+                nc.vector.tensor_scalar(out=result, in0=sums[g][:], scalar1=scale[:, 0:1], scalar2=shift[:, 0:1],
                                         op0=ALU.mult, op1=ALU.add)
-                nc.vector.tensor_scalar_max(out=result[:], in0=result[:], scalar1=0.0)
+                nc.vector.tensor_scalar_max(out=result, in0=result, scalar1=0.0)
             else:
-                nc.scalar.activation(out=result[:], in_=sums[g][:], func=AF.Relu, bias=shift[:, 0:1],
+                nc.scalar.activation(out=result, in_=sums[g][:], func=AF.Relu, bias=shift[:, 0:1],
                                      scale=scale[:, 0:1])
-            nc.sync.dma_start(out=out_view[g], in_=result[:].rearrange("o (b n) -> o b n", b=IMAGES))
+            if g in store_after:
+                first = store_after[g]
+                nc.sync.dma_start(out=store_view[:, IMAGES * first:IMAGES * (g + 1)],
+                                  in_=results[:, first:g + 1].rearrange("o g b n -> o (g b) n"))
             if n < len(again):
                 multiply(again[n], bank_of[g])

@@ -16,6 +16,8 @@ PACK = 4
 GROUPS = 16
 IMAGES = 2
 PIXELS = 256
+GPSIMD_GROUPS = range(4, 16)
+GPSIMD_PIXELS = 96
 RUN = 4
 GROUP_PIXELS = IMAGES * PIXELS
 FLOPS = 2 * 8192 * 1024 * 128
@@ -33,7 +35,7 @@ MX_BEHIND = 1
 
 BY_MATMUL = [(0, 0), (0, 1)]
 
-SCALAR_STATS = [8, 9, 10, 11, 12, 13]
+SCALAR_STATS = [11, 12, 13]
 VECTOR_STATS = GROUPS - len(SCALAR_STATS)
 
 
@@ -48,9 +50,10 @@ def tile_memory_sup_pb_t_kernel(tc, query, concat_memory, conv_w, bn_gamma, bn_b
         keep = ctx.enter_context(tc.tile_pool(name="keep", bufs=1))
         query_pool = ctx.enter_context(tc.tile_pool(name="query_pool", bufs=LOAD_QUERY_AHEAD - QUANTISE_AHEAD + 1))
         memory_pool = ctx.enter_context(tc.tile_pool(name="memory_pool", bufs=LOAD_MEMORY_AHEAD - MEMORY_AHEAD + 1))
-        norm_pool = ctx.enter_context(tc.tile_pool(name="norm_pool", bufs=SQUARE_AHEAD - SPREAD_AHEAD + 1))
+        norm_pool = ctx.enter_context(tc.tile_pool(name="norm_pool", bufs=SQUARE_AHEAD - SPREAD_AHEAD + 2))
         m_pool = ctx.enter_context(tc.tile_pool(name="m_pool", bufs=MEMORY_AHEAD - QUANTISE_AHEAD + 2))
-        q_pool = ctx.enter_context(tc.tile_pool(name="q_pool", bufs=2))
+        q_pool = ctx.enter_context(tc.tile_pool(name="q_pool", bufs=1))
+        spread_pool = ctx.enter_context(tc.tile_pool(name="spread_pool", bufs=3))
         unread_pool = ctx.enter_context(tc.tile_pool(name="unread_pool", bufs=2))
         psum = ctx.enter_context(tc.psum_pool(name="psum", bufs=2))
 
@@ -63,6 +66,7 @@ def tile_memory_sup_pb_t_kernel(tc, query, concat_memory, conv_w, bn_gamma, bn_b
         inv_raw = {}
         inv_norm = {}
         spread = {}
+        spread_sbuf = {}
         q_grouped = {}
         m_grouped = {}
         q_codes = {}
@@ -165,6 +169,10 @@ def tile_memory_sup_pb_t_kernel(tc, query, concat_memory, conv_w, bn_gamma, bn_b
                 inv_norm[g] = norm_pool.tile([P, 2 * IMAGES], F32, name="inv_norm")
             columns = slice(2 * images[0], 2 * images[-1] + 2)
             nc.scalar.activation(out=inv_raw[g][:, columns], in_=squares[g][:, columns], func=AF.Abs_reciprocal_sqrt)
+            if g < 3:
+                clamp_inverse(g, columns)
+
+        def clamp_inverse(g, columns):
             nc.gpsimd.tensor_scalar(out=inv_norm[g][:, columns], in0=inv_raw[g][:, columns], scalar1=1.0 / L2_EPS,
                                     scalar2=0.0, op0=ALU.min, op1=ALU.max)
 
@@ -178,16 +186,28 @@ def tile_memory_sup_pb_t_kernel(tc, query, concat_memory, conv_w, bn_gamma, bn_b
                     nc.tensor.transpose(spread[(g, b)][:, pixels],
                                         inv_norm[g][:, column:column + 1].to_broadcast([P, P]), ident[:])
 
+        def copy_spread(g):
+            spread_sbuf[g] = spread_pool.tile([P, GPSIMD_PIXELS], F32, name="spread_sbuf")
+            nc.scalar.copy(out=spread_sbuf[g][:], in_=spread[(g, 1)][:, PIXELS - GPSIMD_PIXELS:])
+
         def normalise_query(g):
             q_grouped[g] = q_pool.tile([P, IMAGES, PIXELS, PACK], BF16, name="q_grouped", align_bytes=64)
-            for b in range(IMAGES):
-                nc.vector.tensor_tensor(
-                    out=q_grouped[g][:, b].rearrange("p (c i) j -> p c j i", i=RUN),
-                    in0=query_tile[g][:, b].rearrange("p j (c i) -> p c j i", i=RUN),
-                    in1=spread[(g, b)].rearrange("p (c i) -> p c i", i=RUN).unsqueeze(2).to_broadcast(
-                        [P, PIXELS // RUN, PACK, RUN]),
+
+            def multiply_pixels(engine, b, first, last, factor):
+                engine.tensor_tensor(
+                    out=q_grouped[g][:, b, first:last].rearrange("p (c i) j -> p c j i", i=RUN),
+                    in0=query_tile[g][:, b, :, first:last].rearrange("p j (c i) -> p c j i", i=RUN),
+                    in1=factor.rearrange("p (c i) -> p c i", i=RUN).unsqueeze(2).to_broadcast(
+                        [P, (last - first) // RUN, PACK, RUN]),
                     op=ALU.mult,
                 )
+
+            share = GPSIMD_PIXELS if g in GPSIMD_GROUPS else 0
+            split = PIXELS - share
+            if share:
+                multiply_pixels(nc.gpsimd, 1, split, PIXELS, spread_sbuf[g][:])
+            multiply_pixels(nc.vector, 0, 0, PIXELS, spread[(g, 0)])
+            multiply_pixels(nc.vector, 1, 0, split, spread[(g, 1)][:, 0:split])
 
         def quantise_query(g):
             q_codes[g] = keep.tile([P, GROUP_PIXELS], U32, name="q_codes%d" % g, align_bytes=64)
@@ -281,12 +301,16 @@ def tile_memory_sup_pb_t_kernel(tc, query, concat_memory, conv_w, bn_gamma, bn_b
                 load_query(rnd + LOAD_QUERY_AHEAD)
             if 1 < rnd + SPREAD_AHEAD < GROUPS:
                 spread_inv_norm(rnd + SPREAD_AHEAD, both)
+                if rnd + SPREAD_AHEAD in GPSIMD_GROUPS:
+                    copy_spread(rnd + SPREAD_AHEAD)
             if is_group(rnd - MX_BEHIND):
                 multiply(rnd - MX_BEHIND, first_bank(rnd - MX_BEHIND))
             if rnd >= GROUPS - 1:
                 multiply(rnd - (GROUPS - 1), "spread")
             if 0 < rnd + QUANTISE_AHEAD < GROUPS:
                 normalise_query(rnd + QUANTISE_AHEAD)
+            if 3 <= rnd + SQUARE_AHEAD - 1 < GROUPS:
+                clamp_inverse(rnd + SQUARE_AHEAD - 1, slice(0, 2 * IMAGES))
             for b in range(IMAGES):
                 if 1 < rnd + SQUARE_AHEAD < GROUPS:
                     measure_query(rnd + SQUARE_AHEAD, b)

@@ -17,7 +17,7 @@ GROUPS = 16
 IMAGES = 2
 PIXELS = 256
 GPSIMD_GROUPS = range(4, 16)
-GPSIMD_PIXELS = 96
+GPSIMD_PIXELS = 160
 RUN = 4
 GROUP_PIXELS = IMAGES * PIXELS
 FLOPS = 2 * 8192 * 1024 * 128

@@ -35,8 +35,8 @@ MX_BEHIND = 1
 
 BY_MATMUL = [(0, 0), (0, 1)]
 
-SCALAR_STATS = [11, 12, 13]
-VECTOR_STATS = GROUPS - len(SCALAR_STATS)
+SCALAR_STATS = [12, 13, 14]
+VECTOR_STATS = GROUPS - len(SCALAR_STATS) + 1
 
 
 def tile_memory_sup_pb_t_kernel(tc, query, concat_memory, conv_w, bn_gamma, bn_beta, out):
@@ -212,8 +212,14 @@ def tile_memory_sup_pb_t_kernel(tc, query, concat_memory, conv_w, bn_gamma, bn_b
         def quantise_query(g):
             q_codes[g] = keep.tile([P, GROUP_PIXELS], U32, name="q_codes%d" % g, align_bytes=64)
             q_scales[g] = keep.tile([P, GROUP_PIXELS], U8, name="q_scales%d" % g, align_bytes=64)
-            nc.vector.quantize_mx(out=q_codes[g][:].bitcast(FP8X4), scales=q_scales[g][:],
-                                  in_=q_grouped[g][:].rearrange("p b n j -> p (b n j)"))
+            for columns, images in pieces(g):
+                nc.vector.quantize_mx(out=q_codes[g][:, columns].bitcast(FP8X4), scales=q_scales[g][:, columns],
+                                      in_=q_grouped[g][:, images].rearrange("p b n j -> p (b n j)"))
+
+        def pieces(g):
+            if g < GROUPS - 1:
+                return [(slice(0, GROUP_PIXELS), slice(0, IMAGES))]
+            return [(slice(PIXELS * b, PIXELS * b + PIXELS), slice(b, b + 1)) for b in range(IMAGES)]
 
         def turn_memory(g, b):
             turned_m[(g, b)] = psum.tile([P, 2, 2, P], F32, name="turned_m", tag="turned_m")
@@ -239,11 +245,13 @@ def tile_memory_sup_pb_t_kernel(tc, query, concat_memory, conv_w, bn_gamma, bn_b
         def multiply(g, kind):
             sums[g] = psum.tile([P, GROUP_PIXELS], F32, name="sums", tag=kind)
             bank_of[g] = kind
-            nc.tensor.matmul_mx(out=sums[g][:], lhsT=w_codes[:, P:2 * P].bitcast(FP8X4),
-                                lhsT_scale=w_scales[:, P:2 * P],
-                                rhs=m_codes[g][:].bitcast(FP8X4), rhs_scale=m_scales[g][:], start=True, stop=False)
-            nc.tensor.matmul_mx(out=sums[g][:], lhsT=w_codes[:, 0:P].bitcast(FP8X4), lhsT_scale=w_scales[:, 0:P],
-                                rhs=q_codes[g][:].bitcast(FP8X4), rhs_scale=q_scales[g][:], start=False, stop=True)
+            for columns, images in pieces(g):
+                nc.tensor.matmul_mx(out=sums[g][:, columns], lhsT=w_codes[:, P:2 * P].bitcast(FP8X4),
+                                    lhsT_scale=w_scales[:, P:2 * P], rhs=m_codes[g][:, columns].bitcast(FP8X4),
+                                    rhs_scale=m_scales[g][:, columns], start=True, stop=False)
+                nc.tensor.matmul_mx(out=sums[g][:, columns], lhsT=w_codes[:, 0:P].bitcast(FP8X4),
+                                    lhsT_scale=w_scales[:, 0:P], rhs=q_codes[g][:, columns].bitcast(FP8X4),
+                                    rhs_scale=q_scales[g][:, columns], start=False, stop=True)
 
         def first_bank(g):
             if g < GROUPS - 4:
@@ -270,7 +278,8 @@ def tile_memory_sup_pb_t_kernel(tc, query, concat_memory, conv_w, bn_gamma, bn_b
 
         def take_statistics(g):
             slot = g if g < SCALAR_STATS[0] else g - len(SCALAR_STATS)
-            nc.vector.bn_stats(out=stats[:, 6 * slot:6 * slot + 6], in_=sums[g][:])
+            for n, (columns, images) in enumerate(pieces(g)):
+                nc.vector.bn_stats(out=stats[:, 6 * (slot + n):6 * (slot + n) + 6], in_=sums[g][:, columns])
 
         def is_group(g):
             return 0 <= g < GROUPS

from contextlib import ExitStack

import concourse.mybir as mybir
from concourse.masks import make_identity

F32 = mybir.dt.float32
BF16 = mybir.dt.bfloat16
U32 = mybir.dt.uint32
U8 = mybir.dt.uint8
FP8X4 = mybir.dt.float8_e4m3fn_x4
AF = mybir.ActivationFunctionType
ALU = mybir.AluOpType

P = 128
PACK = 4
GROUPS = 16
IMAGES = 2
PIXELS = 256
GPSIMD_GROUPS = range(4, 16)
GPSIMD_PIXELS = 160
RUN = 4
GROUP_PIXELS = IMAGES * PIXELS
FLOPS = 2 * 8192 * 1024 * 128

L2_EPS = 1e-12
BN_EPS = 1e-5

LOAD_QUERY_AHEAD = 7
LOAD_MEMORY_AHEAD = 5
SQUARE_AHEAD = 4
MEMORY_AHEAD = 3
SPREAD_AHEAD = 2
QUANTISE_AHEAD = 1
MX_BEHIND = 1

BY_MATMUL = [(0, 0), (0, 1)]

SCALAR_STATS = [12, 13, 14]
VECTOR_STATS = GROUPS - len(SCALAR_STATS) + 1


def tile_memory_sup_pb_t_kernel(tc, query, concat_memory, conv_w, bn_gamma, bn_beta, out):
    nc = tc.nc
    query_view = query.rearrange("(g b) (p j) h w -> g p b (j h w)", b=IMAGES, j=PACK)
    memory_view = concat_memory.rearrange("(g b p t) k -> g p b (t k)", b=IMAGES, p=P, t=2)

    with ExitStack() as ctx:
        ctx.enter_context(tc.manual_schedule())
        const = ctx.enter_context(tc.tile_pool(name="const", bufs=1))
        keep = ctx.enter_context(tc.tile_pool(name="keep", bufs=1))
        query_pool = ctx.enter_context(tc.tile_pool(name="query_pool", bufs=LOAD_QUERY_AHEAD - QUANTISE_AHEAD + 1))
        memory_pool = ctx.enter_context(tc.tile_pool(name="memory_pool", bufs=LOAD_MEMORY_AHEAD - MEMORY_AHEAD + 1))
        norm_pool = ctx.enter_context(tc.tile_pool(name="norm_pool", bufs=SQUARE_AHEAD - SPREAD_AHEAD + 2))
        m_pool = ctx.enter_context(tc.tile_pool(name="m_pool", bufs=MEMORY_AHEAD - QUANTISE_AHEAD + 2))
        q_pool = ctx.enter_context(tc.tile_pool(name="q_pool", bufs=1))
        spread_pool = ctx.enter_context(tc.tile_pool(name="spread_pool", bufs=3))
        unread_pool = ctx.enter_context(tc.tile_pool(name="unread_pool", bufs=2))
        psum = ctx.enter_context(tc.psum_pool(name="psum", bufs=2))

        query_tile = {}
        memory_tile = {}
        turned_q = {}
        gram = {}
        turned_m = {}
        squares = {}
        inv_raw = {}
        inv_norm = {}
        spread = {}
        spread_sbuf = {}
        q_grouped = {}
        m_grouped = {}
        q_codes = {}
        q_scales = {}
        m_codes = {}
        m_scales = {}
        sums = {}
        bank_of = {}

        one = const.tile([P, 1], F32, name="one")
        nc.vector.memset(one[:], 1.0)
        warm = const.tile([P, 1], F32, name="warm")
        nc.scalar.activation(out=warm[:], in_=one[:], func=AF.Abs_reciprocal_sqrt)
        ident = const.tile([P, P], F32, name="ident")
        make_identity(nc, ident[:])
        gamma = const.tile([P, 1], BF16, name="gamma")
        beta = const.tile([P, 1], BF16, name="beta")
        with nc.allow_non_contiguous_dma(reason="one bn parameter per partition"):
            nc.gpsimd.dma_start(out=gamma[:], in_=bn_gamma.rearrange("(o x) -> o x", x=1))
            nc.gpsimd.dma_start(out=beta[:], in_=bn_beta.rearrange("(o x) -> o x", x=1))
        stats = const.tile([P, 6 * VECTOR_STATS + 3 * len(SCALAR_STATS)], F32, name="stats")
        scalar_triples = stats[:, 6 * VECTOR_STATS:].rearrange("p (k s) -> p k s", s=3)
        nc.vector.memset(scalar_triples, float(GROUP_PIXELS))
        totals = const.tile([P, len(SCALAR_STATS)], F32, name="totals")
        deviations = const.tile([P, len(SCALAR_STATS)], F32, name="deviations")
        w_tile = const.tile([P, 1024], BF16, name="w_tile")
        w_grouped = const.tile([P, 2, P, PACK], BF16, name="w_grouped", align_bytes=64)
        w_codes = const.tile([P, 2 * P], U32, name="w_codes", align_bytes=64)
        w_scales = const.tile([P, 2 * P], U8, name="w_scales", align_bytes=64)
        turned_w = psum.tile([P, 4, P], F32, name="turned_w", tag="sums")

        def load_query(g):
            query_tile[g] = query_pool.tile([P, IMAGES, PACK, PIXELS], BF16, name="query_tile")
            dst = query_tile[g][:].rearrange("p b j n -> p b (j n)")
            if g == 0:
                for b in range(IMAGES):
                    nc.sync.dma_start(out=dst[:, b], in_=query_view[g][:, b])
            else:
                nc.sync.dma_start(out=dst, in_=query_view[g])

        def load_memory(g):
            memory_tile[g] = memory_pool.tile([P, IMAGES, 2, 512], BF16, name="memory_tile")
            nc.sync.dma_start(out=memory_tile[g][:].rearrange("p b t k -> p b (t k)"), in_=memory_view[g])

        def turn_weights():
            words = w_tile[:].bitcast(F32)
            for h in range(2):
                nc.tensor.transpose(turned_w[:, h, :], words[:, h:256:2], ident[:])
            for u in range(2):
                nc.tensor.transpose(turned_w[:, 2 + u, :], words[:, 256 + u:512:2], ident[:])

        def quantise_weights():
            nc.vector.tensor_copy(out=w_grouped[:].bitcast(F32),
                                  in_=turned_w[:].rearrange("p (a h) o -> p a o h", a=2))
            nc.vector.quantize_mx(out=w_codes[:].bitcast(FP8X4), scales=w_scales[:],
                                  in_=w_grouped[:].rearrange("p a o t -> p (a o t)"))

        def measure_query(g, b):
            if (g, b) in BY_MATMUL:
                gram_query(g, b)
                sum_squares_from_gram(g, b)
            else:
                turn_query(g, b)
                sum_squares(g, b)

        def turn_query(g, b):
            turned_q[(g, b)] = psum.tile([P, PACK, P], F32, name="turned_q", tag="turned_q")
            words = query_tile[g][:].bitcast(F32)
            for j in range(PACK):
                nc.tensor.transpose(turned_q[(g, b)][:, j, :], words[:, b, j, :], ident[:])

        def sum_squares(g, b):
            if b == 0:
                squares[g] = norm_pool.tile([P, 2 * IMAGES], F32, name="squares")
            halves = turned_q[(g, b)][:].bitcast(BF16).rearrange("w j (p e) -> w j p e", e=2)
            for parity in range(2):
                unread = unread_pool.tile([P, PACK, P], BF16, name="unread")
                nc.scalar.activation(out=unread[:], in_=halves[:, :, :, parity], func=AF.Square,
                                     accum_out=squares[g][:, 2 * b + parity:2 * b + parity + 1])

        def gram_query(g, b):
            gram[(g, b)] = psum.tile([P, 2, P], F32, name="gram", tag="turned_q")
            for h in range(2):
                for j in range(PACK):
                    pixels = query_tile[g][:, b, j, P * h:P * h + P]
                    nc.tensor.matmul(gram[(g, b)][:, h, :], lhsT=pixels, rhs=pixels, start=(j == 0), stop=(j == PACK - 1))

        def sum_squares_from_gram(g, b):
            if b == 0:
                squares[g] = norm_pool.tile([P, 2 * IMAGES], F32, name="squares")
            for h in range(2):
                unread_diagonal = unread_pool.tile([P, P], F32, name="unread_diagonal")
                nc.vector.scalar_tensor_tensor(out=unread_diagonal[:], in0=gram[(g, b)][:, h, :], scalar=1.0, in1=ident[:],
                                               op0=ALU.mult, op1=ALU.mult,
                                               accum_out=squares[g][:, 2 * b + h:2 * b + h + 1])

        def invert_norm(g, images):
            if images[0] == 0:
                inv_raw[g] = norm_pool.tile([P, 2 * IMAGES], F32, name="inv_raw")
                inv_norm[g] = norm_pool.tile([P, 2 * IMAGES], F32, name="inv_norm")
            columns = slice(2 * images[0], 2 * images[-1] + 2)
            nc.scalar.activation(out=inv_raw[g][:, columns], in_=squares[g][:, columns], func=AF.Abs_reciprocal_sqrt)
            if g < 3:
                clamp_inverse(g, columns)

        def clamp_inverse(g, columns):
            nc.gpsimd.tensor_scalar(out=inv_norm[g][:, columns], in0=inv_raw[g][:, columns], scalar1=1.0 / L2_EPS,
                                    scalar2=0.0, op0=ALU.min, op1=ALU.max)

        def spread_inv_norm(g, images):
            spread_tile = psum.tile([P, len(images), PIXELS], F32, name="spread_tile", tag="spread")
            for b in images:
                spread[(g, b)] = spread_tile[:, b - images[0]]
                for half in range(2):
                    column = 2 * b + half
                    pixels = slice(P * half, P * half + P) if (g, b) in gram else slice(half, PIXELS, 2)
                    nc.tensor.transpose(spread[(g, b)][:, pixels],
                                        inv_norm[g][:, column:column + 1].to_broadcast([P, P]), ident[:])

        def copy_spread(g):
            spread_sbuf[g] = spread_pool.tile([P, GPSIMD_PIXELS], F32, name="spread_sbuf")
            nc.scalar.copy(out=spread_sbuf[g][:], in_=spread[(g, 1)][:, PIXELS - GPSIMD_PIXELS:])

        def normalise_query(g):
            q_grouped[g] = q_pool.tile([P, IMAGES, PIXELS, PACK], BF16, name="q_grouped", align_bytes=64)

            def multiply_pixels(engine, b, first, last, factor):
                engine.tensor_tensor(
                    out=q_grouped[g][:, b, first:last].rearrange("p (c i) j -> p c j i", i=RUN),
                    in0=query_tile[g][:, b, :, first:last].rearrange("p j (c i) -> p c j i", i=RUN),
                    in1=factor.rearrange("p (c i) -> p c i", i=RUN).unsqueeze(2).to_broadcast(
                        [P, (last - first) // RUN, PACK, RUN]),
                    op=ALU.mult,
                )

            share = GPSIMD_PIXELS if g in GPSIMD_GROUPS else 0
            split = PIXELS - share
            if share:
                multiply_pixels(nc.gpsimd, 1, split, PIXELS, spread_sbuf[g][:])
            multiply_pixels(nc.vector, 0, 0, PIXELS, spread[(g, 0)])
            multiply_pixels(nc.vector, 1, 0, split, spread[(g, 1)][:, 0:split])

        def quantise_query(g):
            q_codes[g] = keep.tile([P, GROUP_PIXELS], U32, name="q_codes%d" % g, align_bytes=64)
            q_scales[g] = keep.tile([P, GROUP_PIXELS], U8, name="q_scales%d" % g, align_bytes=64)
            for columns, images in pieces(g):
                nc.vector.quantize_mx(out=q_codes[g][:, columns].bitcast(FP8X4), scales=q_scales[g][:, columns],
                                      in_=q_grouped[g][:, images].rearrange("p b n j -> p (b n j)"))

        def pieces(g):
            if g < GROUPS - 1:
                return [(slice(0, GROUP_PIXELS), slice(0, IMAGES))]
            return [(slice(PIXELS * b, PIXELS * b + PIXELS), slice(b, b + 1)) for b in range(IMAGES)]

        def turn_memory(g, b):
            turned_m[(g, b)] = psum.tile([P, 2, 2, P], F32, name="turned_m", tag="turned_m")
            words = memory_tile[g][:].bitcast(F32)
            for t in range(2):
                for u in range(2):
                    nc.tensor.transpose(turned_m[(g, b)][:, u, t, :], words[:, b, t, u:256:2], ident[:])

        def group_memory(g, b):
            if b == 0:
                m_grouped[g] = m_pool.tile([P, IMAGES, PIXELS, PACK], BF16, name="m_grouped", align_bytes=64)
            nc.scalar.copy(
                out=m_grouped[g][:].bitcast(F32)[:, b].rearrange("p (r t) u -> p r t u", t=2),
                in_=turned_m[(g, b)][:].rearrange("p u t r -> p r t u"),
            )

        def quantise_memory(g):
            m_codes[g] = keep.tile([P, GROUP_PIXELS], U32, name="m_codes%d" % g, align_bytes=64)
            m_scales[g] = keep.tile([P, GROUP_PIXELS], U8, name="m_scales%d" % g, align_bytes=64)
            nc.vector.quantize_mx(out=m_codes[g][:].bitcast(FP8X4), scales=m_scales[g][:],
                                  in_=m_grouped[g][:].rearrange("p b n j -> p (b n j)"))

        def multiply(g, kind):
            sums[g] = psum.tile([P, GROUP_PIXELS], F32, name="sums", tag=kind)
            bank_of[g] = kind
            for columns, images in pieces(g):
                nc.tensor.matmul_mx(out=sums[g][:, columns], lhsT=w_codes[:, P:2 * P].bitcast(FP8X4),
                                    lhsT_scale=w_scales[:, P:2 * P], rhs=m_codes[g][:, columns].bitcast(FP8X4),
                                    rhs_scale=m_scales[g][:, columns], start=True, stop=False)
                nc.tensor.matmul_mx(out=sums[g][:, columns], lhsT=w_codes[:, 0:P].bitcast(FP8X4),
                                    lhsT_scale=w_scales[:, 0:P], rhs=q_codes[g][:, columns].bitcast(FP8X4),
                                    rhs_scale=q_scales[g][:, columns], start=False, stop=True)

        def first_bank(g):
            if g < GROUPS - 4:
                return "sums"
            if g < GROUPS - 2:
                return "turned_q"
            return "turned_m"

        def sum_group(g):
            k = SCALAR_STATS.index(g)
            unread = unread_pool.tile([P, GROUP_PIXELS], BF16, name="unread")
            nc.scalar.activation(out=unread[:], in_=sums[g][:], func=AF.Identity, accum_out=totals[:, k:k + 1])

        def sum_deviations(g):
            k = SCALAR_STATS.index(g)
            unread = unread_pool.tile([P, GROUP_PIXELS], BF16, name="unread")
            nc.scalar.activation(out=unread[:], in_=sums[g][:], func=AF.Square, scale=-float(GROUP_PIXELS),
                                 bias=totals[:, k:k + 1], accum_out=deviations[:, k:k + 1])

        def gather_statistics():
            nc.vector.tensor_scalar_mul(out=scalar_triples[:, :, 1], in0=totals[:], scalar1=1.0 / GROUP_PIXELS)
            nc.vector.tensor_scalar_mul(out=scalar_triples[:, :, 2], in0=deviations[:],
                                        scalar1=1.0 / (GROUP_PIXELS * GROUP_PIXELS))

        def take_statistics(g):
            slot = g if g < SCALAR_STATS[0] else g - len(SCALAR_STATS)
            for n, (columns, images) in enumerate(pieces(g)):
                nc.vector.bn_stats(out=stats[:, 6 * (slot + n):6 * (slot + n) + 6], in_=sums[g][:, columns])

        def is_group(g):
            return 0 <= g < GROUPS

        both = range(IMAGES)
        load_query(0)
        load_query(1)
        nc.sync.dma_start(out=w_tile[:], in_=conv_w)
        load_memory(0)
        for b in both:
            measure_query(0, b)
            invert_norm(0, [b])
        measure_query(1, 0)
        spread_inv_norm(0, [0])
        spread_inv_norm(0, [1])
        measure_query(1, 1)
        invert_norm(1, both)
        turn_weights()
        normalise_query(0)
        quantise_weights()
        for b in both:
            turn_memory(0, b)
            group_memory(0, b)
        for rnd in range(-LOAD_QUERY_AHEAD, GROUPS + MX_BEHIND):
            if 0 < rnd + LOAD_MEMORY_AHEAD < GROUPS:
                load_memory(rnd + LOAD_MEMORY_AHEAD)
            if 1 < rnd + LOAD_QUERY_AHEAD < GROUPS:
                load_query(rnd + LOAD_QUERY_AHEAD)
            if 1 < rnd + SPREAD_AHEAD < GROUPS:
                spread_inv_norm(rnd + SPREAD_AHEAD, both)
                if rnd + SPREAD_AHEAD in GPSIMD_GROUPS:
                    copy_spread(rnd + SPREAD_AHEAD)
            if is_group(rnd - MX_BEHIND):
                multiply(rnd - MX_BEHIND, first_bank(rnd - MX_BEHIND))
            if rnd >= GROUPS - 1:
                multiply(rnd - (GROUPS - 1), "spread")
            if 0 < rnd + QUANTISE_AHEAD < GROUPS:
                normalise_query(rnd + QUANTISE_AHEAD)
            if 3 <= rnd + SQUARE_AHEAD - 1 < GROUPS:
                clamp_inverse(rnd + SQUARE_AHEAD - 1, slice(0, 2 * IMAGES))
            for b in range(IMAGES):
                if 1 < rnd + SQUARE_AHEAD < GROUPS:
                    measure_query(rnd + SQUARE_AHEAD, b)
                if rnd + SQUARE_AHEAD == 2 and b == 0:
                    spread_inv_norm(1, both)
                if b == 1 and rnd - MX_BEHIND in SCALAR_STATS:
                    sum_group(rnd - MX_BEHIND)
                if 0 < rnd + MEMORY_AHEAD < GROUPS:
                    turn_memory(rnd + MEMORY_AHEAD, b)
                    group_memory(rnd + MEMORY_AHEAD, b)
            if 1 < rnd + SQUARE_AHEAD < GROUPS:
                invert_norm(rnd + SQUARE_AHEAD, both)
            if is_group(rnd + QUANTISE_AHEAD):
                if rnd + QUANTISE_AHEAD == 0:
                    quantise_query(0)
                    quantise_memory(0)
                else:
                    quantise_memory(rnd + QUANTISE_AHEAD)
                    quantise_query(rnd + QUANTISE_AHEAD)
            if rnd - MX_BEHIND in SCALAR_STATS:
                if rnd - MX_BEHIND == SCALAR_STATS[-1]:
                    sum_deviations(SCALAR_STATS[-2])
                if rnd - MX_BEHIND != SCALAR_STATS[-2]:
                    sum_deviations(rnd - MX_BEHIND)
            elif is_group(rnd - MX_BEHIND):
                if rnd - MX_BEHIND == GROUPS - 1:
                    gather_statistics()
                take_statistics(rnd - MX_BEHIND)

        mean_var = const.tile([P, 2], F32, name="mean_var")
        nc.vector.bn_aggr(out=mean_var[:], in_=stats[:])
        neg_mean_gamma = const.tile([P, 1], F32, name="neg_mean_gamma")
        nc.vector.scalar_tensor_tensor(out=neg_mean_gamma[:], in0=mean_var[:, 0:1], scalar=-1.0, in1=gamma[:],
                                       op0=ALU.mult, op1=ALU.mult)
        rstd = const.tile([P, 1], F32, name="rstd")
        nc.scalar.activation(out=rstd[:], in_=mean_var[:, 1:2], func=AF.Abs_reciprocal_sqrt, bias=BN_EPS)
        scale = const.tile([P, 1], F32, name="scale")
        nc.scalar.mul(out=scale[:], in_=gamma[:], mul=rstd[:, 0:1])
        shift = const.tile([P, 1], F32, name="shift")
        nc.scalar.activation(out=shift[:], in_=neg_mean_gamma[:], func=AF.Identity, bias=beta[:, 0:1], scale=rstd[:, 0:1])

        in_psum = list(range(GROUPS - 6, GROUPS)) + [0, 1]
        again = list(range(2, GROUPS - 6))
        store_view = out.rearrange("n o h w -> o n (h w)")
        store_after = {10: 10, 11: 11, 13: 12, 15: 14, 1: 0, 5: 2, 9: 6}
        results = keep.tile([P, GROUPS, IMAGES, PIXELS], F32, name="results")
        for n, g in enumerate(in_psum + again):
            result = results[:, g].rearrange("o b n -> o (b n)")
            if n % 3 == 1:
                nc.vector.tensor_scalar(out=result, in0=sums[g][:], scalar1=scale[:, 0:1], scalar2=shift[:, 0:1],
                                        op0=ALU.mult, op1=ALU.add)
                nc.vector.tensor_scalar_max(out=result, in0=result, scalar1=0.0)
            else:
                nc.scalar.activation(out=result, in_=sums[g][:], func=AF.Relu, bias=shift[:, 0:1],
                                     scale=scale[:, 0:1])
            if g in store_after:
                first = store_after[g]
                nc.sync.dma_start(out=store_view[:, IMAGES * first:IMAGES * (g + 1)],
                                  in_=results[:, first:g + 1].rearrange("o g b n -> o (g b) n"))
            if n < len(again):
                multiply(again[n], bank_of[g])
